import numpy as np
import ml_dtypes


def mxq(x, axis, fmt="e4m3"):
    dtype, down = {"e4m3": (ml_dtypes.float8_e4m3fn, 7), "e5m2": (ml_dtypes.float8_e5m2, 14)}[fmt]
    v = np.moveaxis(np.asarray(x, np.float32).astype(ml_dtypes.bfloat16).astype(np.float64), axis, -1)
    blocks = v.reshape(v.shape[:-1] + (-1, 32))
    amax = np.abs(blocks).max(-1, keepdims=True)
    byte = np.maximum(np.where(amax > 0, np.frexp(amax)[1] - 1 + 127, 0) - down, 1)
    scale = np.exp2(byte - 127.0)
    codes = (blocks / scale).astype(np.float32).astype(dtype).astype(np.float64)
    return np.moveaxis((codes * scale).reshape(v.shape), -1, axis)


WIDE = False


def mx_kscale(k):
    if not WIDE:
        return np.ones(k)
    levels = np.array([30, -30])
    if k % 512:
        return np.exp2(np.random.permutation(np.resize(levels, k // 32))).repeat(32)
    a = np.empty((k // 512, 16))
    for p in range(k // 512):
        a[p, :8] = np.random.permutation(np.resize(levels, 8))
        for g in range(8):
            far = levels[np.abs(levels - a[p, g]) >= 10]
            a[p, g + 8] = far[np.random.randint(len(far))]
    return np.exp2(a.ravel()).repeat(32)


BF16 = ml_dtypes.bfloat16


def bf(x):
    return np.asarray(x, np.float32).astype(BF16)


def f64(x):
    return np.asarray(x).astype(np.float64)


B, S, D, H, DH = 2, 256, 2048, 16, 128
E = H * DH
EPS = 1e-6
MU = 0.5


def setup_inputs():
    s = mx_kscale(D)
    g = np.random.standard_normal((D, H, DH))
    g = (g - g.mean(-1, keepdims=True)) / np.sqrt(D * (1.0 + MU * MU))
    lev = 2.5 + np.random.random((1, H, 1))
    w = (g + lev / (D * MU * DH)).reshape(D, E)
    x = np.random.standard_normal((B, S, D)) + MU
    return {"x": bf(x * s), "w": bf(w / s[:, None])}


def reference(x, w):
    y = mxq(f64(x), 2, "e5m2") @ mxq(f64(w), 0, "e4m3")
    yh = y.reshape(B, S, H, DH).transpose(0, 2, 1, 3)
    return yh / (yh.sum(-1, keepdims=True) + EPS)

@@ -1,0 +1,221 @@
+from contextlib import ExitStack
+
+import concourse.mybir as mybir
+from concourse.masks import make_identity
+
+B, S, D, H, DH = 2, 256, 2048, 16, 128
+EPS = 1e-6
+FLOPS = 2 * B * S * D * H * DH
+
+F32 = mybir.dt.float32
+BF16 = mybir.dt.bfloat16
+U32 = mybir.dt.uint32
+U8 = mybir.dt.uint8
+E4X4 = mybir.dt.float8_e4m3fn_x4
+E5X4 = mybir.dt.float8_e5m2_x4
+ADD = mybir.AluOpType.add
+MULT = mybir.AluOpType.mult
+COPY = mybir.ActivationFunctionType.Copy
+AX = mybir.AxisListType.X
+
+P = 128
+PACK = 4
+KP = P * PACK
+G = D // KP
+NT = 512
+J = H * DH // NT
+HT = NT // DH
+E2 = S // P
+M = B * E2
+U = J * G
+CV = 288
+
+
+def tile_multiheadattention_pa_kernel(tc, x, w, out):
+    nc = tc.nc
+    with ExitStack() as ctx:
+        const = ctx.enter_context(tc.tile_pool(name="const", bufs=1))
+        xraw_pool = ctx.enter_context(tc.tile_pool(name="xraw", bufs=M))
+        wraw_pool = ctx.enter_context(tc.tile_pool(name="wraw", bufs=U))
+        xg_pool = ctx.enter_context(tc.tile_pool(name="xg", bufs=2))
+        wg_pool = ctx.enter_context(tc.tile_pool(name="wg", bufs=3))
+        keep = ctx.enter_context(tc.tile_pool(name="keep", bufs=1))
+        stat_pool = ctx.enter_context(tc.tile_pool(name="stat", bufs=3))
+        res_pool = ctx.enter_context(tc.tile_pool(name="res", bufs=3))
+        psum = ctx.enter_context(tc.psum_pool(name="psum", bufs=8))
+
+        ident = const.tile([P, P], F32, name="ident")
+        make_identity(nc, ident[:])
+        warm_in = const.tile([P, 1], F32, name="warm_in")
+        warm_out = const.tile([P, 1], F32, name="warm_out")
+        nc.gpsimd.memset(warm_in[:], 0.0)
+        nc.scalar.activation(out=warm_out[:], in_=warm_in[:], func=COPY)
+
+        xc = keep.tile([P, M, G * P], U32, name="xc", align_bytes=64)
+        xs = keep.tile([P, M, G * P], U8, name="xs", align_bytes=64)
+        wc = [keep.tile([P, G, NT], U32, name="wc%d" % j, align_bytes=64) for j in range(J)]
+        ws = [keep.tile([P, G, NT], U8, name="ws%d" % j, align_bytes=64) for j in range(J)]
+
+        ctx.enter_context(tc.manual_schedule())
+
+        xraw = []
+        for m in range(M):
+            b, e = divmod(m, E2)
+            t = xraw_pool.tile([P, D], BF16, name="xraw")
+            nc.sync.dma_start(out=t[:], in_=x[b].rearrange("(p e) k -> p e k", e=E2)[:, e, :])
+            xraw.append(t)
+        wraw = []
+        for u in range(U):
+            j, g = divmod(u, G)
+            t = wraw_pool.tile([P, PACK, NT], BF16, name="wraw")
+            nc.sync.dma_start(
+                out=t[:],
+                in_=w[g * KP : (g + 1) * KP, j * NT : (j + 1) * NT].rearrange("(p t) c -> p t c", t=PACK),
+            )
+            wraw.append(t)
+
+        for m in range(M):
+            words = xraw[m][:].bitcast(F32)
+            xg = xg_pool.tile([P, G, P, PACK], BF16, name="xg", align_bytes=64)
+            xg_flat = xg[:].rearrange("p g r t -> p (g r t)")
+            xg_words = xg_flat.bitcast(F32).rearrange("p (g r u) -> p g r u", g=G, u=2)
+            for half in range(2):
+                bank = psum.tile([P, 2, 2, P], F32, name="bank")
+                for gg in range(2):
+                    base = (KP // 2) * (2 * half + gg)
+                    for u2 in range(2):
+                        nc.tensor.transpose(
+                            bank[:, gg, u2, :], words[:, base + u2 : base + KP // 2 : 2], ident[:]
+                        )
+                dst = xg_words[:, 2 * half : 2 * half + 2, :, :]
+                src = bank[:].rearrange("p g u r -> p g r u")
+                if half == 0:
+                    nc.vector.tensor_copy(out=dst, in_=src)
+                else:
+                    nc.scalar.copy(out=dst, in_=src)
+            nc.vector.quantize_mx(out=xc[:, m, :].bitcast(E5X4), scales=xs[:, m, :], in_=xg_flat)
+
+        wg = {}
+        acc = {}
+        sums = {}
+        recs = {}
+        res = {}
+
+        def interleave(u):
+            t = wg_pool.tile([P, NT, PACK], BF16, name="wg", align_bytes=64)
+            wg[u] = t
+            src = wraw[u][:].rearrange("p t c -> p c t")
+            nc.vector.tensor_copy(out=t[:, 0:CV, :], in_=src[:, 0:CV, :])
+            nc.scalar.copy(out=t[:, CV:NT, :], in_=src[:, CV:NT, :])
+
+        def quantise(u):
+            j, g = divmod(u, G)
+            nc.vector.quantize_mx(
+                out=wc[j][:, g, :].bitcast(E4X4),
+                scales=ws[j][:, g, :],
+                in_=wg[u][:].rearrange("p c t -> p (c t)"),
+            )
+
+        def multiply(u):
+            j, g = divmod(u, G)
+            for m in range(M):
+                if g == 0:
+                    acc[(j, m)] = psum.tile([P, NT], F32, name="bank")
+                cols = slice(g * P, (g + 1) * P)
+                nc.tensor.matmul_mx(
+                    out=acc[(j, m)][:],
+                    lhsT=xc[:, m, cols].bitcast(E5X4),
+                    lhsT_scale=xs[:, m, cols],
+                    rhs=wc[j][:, g, :].bitcast(E4X4),
+                    rhs_scale=ws[j][:, g, :],
+                    start=(g == 0),
+                    stop=(g == G - 1),
+                )
+
+        def head_sums(j, b, e):
+            if e == 0:
+                sums[(j, b)] = stat_pool.tile([P, E2 * HT], F32, name="sums")
+            nc.vector.tensor_reduce(
+                out=sums[(j, b)][:, e * HT : (e + 1) * HT],
+                in_=acc[(j, b * E2 + e)][:].rearrange("p (h d) -> p h d", h=HT),
+                axis=AX,
+                op=ADD,
+            )
+
+        def add_eps(j, b):
+            nc.vector.tensor_scalar_add(out=sums[(j, b)][:], in0=sums[(j, b)][:], scalar1=EPS)
+
+        def invert(j, b):
+            recs[(j, b)] = stat_pool.tile([P, E2 * HT], F32, name="recs")
+            nc.vector.reciprocal(out=recs[(j, b)][:], in_=sums[(j, b)][:])
+
+        def scale_on_scalar(j, b, e):
+            if (j, b) not in res:
+                res[(j, b)] = res_pool.tile([P, HT, E2, DH], F32, name="res")
+            for h in range(HT):
+                nc.scalar.activation(
+                    out=res[(j, b)][:, h, e, :],
+                    in_=acc[(j, b * E2 + e)][:, h * DH : (h + 1) * DH],
+                    func=COPY,
+                    scale=recs[(j, b)][:, e * HT + h : e * HT + h + 1],
+                )
+
+        def scale_on_vector(j, b, e):
+            if (j, b) not in res:
+                res[(j, b)] = res_pool.tile([P, HT, E2, DH], F32, name="res")
+            nc.vector.tensor_tensor(
+                out=res[(j, b)][:, :, e, :],
+                in0=acc[(j, b * E2 + e)][:].rearrange("p (h d) -> p h d", h=HT),
+                in1=recs[(j, b)][:, e * HT : (e + 1) * HT].unsqueeze(2).to_broadcast([P, HT, DH]),
+                op=MULT,
+            )
+
+        def store(j, b):
+            nc.sync.dma_start(
+                out=out[b, j * HT : (j + 1) * HT].rearrange("h (p e) d -> p h (e d)", e=E2),
+                in_=res[(j, b)][:].rearrange("p h e d -> p h (e d)"),
+            )
+
+        def pair_of(step):
+            if step < G or step % 2 == 1:
+                return None
+            k = (step - G) // 2
+            return divmod(k, B) if k < J * B else None
+
+        interleave(0)
+        for u in range(U):
+            if u + 1 < U:
+                interleave(u + 1)
+            now, one, two = pair_of(u), pair_of(u - 1), pair_of(u - 2)
+            if now:
+                head_sums(now[0], now[1], 0)
+                head_sums(now[0], now[1], 1)
+            if one:
+                invert(one[0], one[1])
+            quantise(u)
+            if now:
+                add_eps(now[0], now[1])
+            if one:
+                scale_on_scalar(one[0], one[1], 0)
+            if two:
+                scale_on_scalar(two[0], two[1], 1)
+                store(two[0], two[1])
+            multiply(u)
+
+        L = J - 1
+        scale_on_scalar(L - 1, 1, 1)
+        store(L - 1, 1)
+        head_sums(L, 0, 0)
+        head_sums(L, 0, 1)
+        head_sums(L, 1, 0)
+        add_eps(L, 0)
+        head_sums(L, 1, 1)
+        invert(L, 0)
+        add_eps(L, 1)
+        scale_on_scalar(L, 0, 0)
+        scale_on_vector(L, 0, 1)
+        store(L, 0)
+        invert(L, 1)
+        scale_on_scalar(L, 1, 0)
+        scale_on_vector(L, 1, 1)
+        store(L, 1)

@@ -28,7 +28,9 @@ HT = NT // DH
 E2 = S // P
 M = B * E2
 U = J * G
-CV = 288
+CV = 208
+CS = 112
+CP = NT - CV - CS
 
 
 def tile_multiheadattention_pa_kernel(tc, x, w, out):
@@ -41,11 +43,14 @@ def tile_multiheadattention_pa_kernel(tc, x, w, out):
         wg_pool = ctx.enter_context(tc.tile_pool(name="wg", bufs=3))
         keep = ctx.enter_context(tc.tile_pool(name="keep", bufs=1))
         stat_pool = ctx.enter_context(tc.tile_pool(name="stat", bufs=3))
-        res_pool = ctx.enter_context(tc.tile_pool(name="res", bufs=3))
-        psum = ctx.enter_context(tc.psum_pool(name="psum", bufs=8))
+        res_pool = ctx.enter_context(tc.tile_pool(name="res", bufs=J * B))
+        psum = ctx.enter_context(tc.psum_pool(name="psum", bufs=7))
+        stage_pool = ctx.enter_context(tc.psum_pool(name="stagep", bufs=1))
 
         ident = const.tile([P, P], F32, name="ident")
         make_identity(nc, ident[:])
+        ident_bf = const.tile([P, P], BF16, name="ident_bf")
+        make_identity(nc, ident_bf[:])
         warm_in = const.tile([P, 1], F32, name="warm_in")
         warm_out = const.tile([P, 1], F32, name="warm_out")
         nc.gpsimd.memset(warm_in[:], 0.0)
@@ -101,12 +106,35 @@ def tile_multiheadattention_pa_kernel(tc, x, w, out):
         recs = {}
         res = {}
 
+        stage = {}
+
+        def stage_on_tensor(u):
+            t = stage_pool.tile([P, 2 * NT], BF16, name="stage")
+            stage[u] = t
+            src = wraw[u][:].rearrange("p t c -> p c t")
+            for c0 in range(0, CP, P):
+                n = min(P, CP - c0)
+                nc.tensor.matmul(
+                    out=t[:, c0 * PACK : (c0 + n) * PACK].rearrange("p (c t) -> p c t", t=PACK),
+                    lhsT=ident_bf[:],
+                    rhs=src[:, CV + CS + c0 : CV + CS + c0 + n, :],
+                    start=True,
+                    stop=True,
+                )
+
         def interleave(u):
             t = wg_pool.tile([P, NT, PACK], BF16, name="wg", align_bytes=64)
             wg[u] = t
             src = wraw[u][:].rearrange("p t c -> p c t")
+            nc.scalar.copy(
+                out=t[:, CV + CS : NT, :],
+                in_=stage[u][:, 0 : CP * PACK].rearrange("p (c t) -> p c t", t=PACK),
+            )
             nc.vector.tensor_copy(out=t[:, 0:CV, :], in_=src[:, 0:CV, :])
-            nc.scalar.copy(out=t[:, CV:NT, :], in_=src[:, CV:NT, :])
+            for k in pending:
+                store(k[0], k[1], nc.scalar)
+            pending.clear()
+            nc.scalar.copy(out=t[:, CV : CV + CS, :], in_=src[:, CV : CV + CS, :])
 
         def quantise(u):
             j, g = divmod(u, G)
@@ -116,9 +144,9 @@ def tile_multiheadattention_pa_kernel(tc, x, w, out):
                 in_=wg[u][:].rearrange("p c t -> p (c t)"),
             )
 
-        def multiply(u):
-            j, g = divmod(u, G)
-            for m in range(M):
+        def multiply(j, b, g):
+            for e in range(E2):
+                m = b * E2 + e
                 if g == 0:
                     acc[(j, m)] = psum.tile([P, NT], F32, name="bank")
                 cols = slice(g * P, (g + 1) * P)
@@ -142,8 +170,8 @@ def tile_multiheadattention_pa_kernel(tc, x, w, out):
                 op=ADD,
             )
 
-        def add_eps(j, b):
-            nc.vector.tensor_scalar_add(out=sums[(j, b)][:], in0=sums[(j, b)][:], scalar1=EPS)
+        def add_eps(j, b, eng):
+            eng.tensor_scalar(out=sums[(j, b)][:], in0=sums[(j, b)][:], scalar1=EPS, scalar2=None, op0=ADD)
 
         def invert(j, b):
             recs[(j, b)] = stat_pool.tile([P, E2 * HT], F32, name="recs")
@@ -170,8 +198,8 @@ def tile_multiheadattention_pa_kernel(tc, x, w, out):
                 op=MULT,
             )
 
-        def store(j, b):
-            nc.sync.dma_start(
+        def store(j, b, eng):
+            eng.dma_start(
                 out=out[b, j * HT : (j + 1) * HT].rearrange("h (p e) d -> p h (e d)", e=E2),
                 in_=res[(j, b)][:].rearrange("p h e d -> p h (e d)"),
             )
@@ -182,10 +210,17 @@ def tile_multiheadattention_pa_kernel(tc, x, w, out):
             k = (step - G) // 2
             return divmod(k, B) if k < J * B else None
 
+        pending = []
+        L = J - 1
+        stage_on_tensor(0)
         interleave(0)
+        stage_on_tensor(1)
         for u in range(U):
+            j, g = divmod(u, G)
             if u + 1 < U:
                 interleave(u + 1)
+            if u + 2 < U:
+                stage_on_tensor(u + 2)
             now, one, two = pair_of(u), pair_of(u - 1), pair_of(u - 2)
             if now:
                 head_sums(now[0], now[1], 0)
@@ -194,28 +229,37 @@ def tile_multiheadattention_pa_kernel(tc, x, w, out):
                 invert(one[0], one[1])
             quantise(u)
             if now:
-                add_eps(now[0], now[1])
+                add_eps(now[0], now[1], nc.gpsimd)
             if one:
                 scale_on_scalar(one[0], one[1], 0)
             if two:
                 scale_on_scalar(two[0], two[1], 1)
-                store(two[0], two[1])
-            multiply(u)
+                pending.append(two)
+            multiply(j, 0, g)
+            if u >= 2 and u < U - 2:
+                multiply((u - 2) // G, 1, (u - 2) % G)
+            if u == U - 2:
+                multiply(L, 1, 0)
+                multiply(L, 1, 1)
+                multiply(L, 1, 2)
+            if u == U - 1:
+                multiply(L, 1, 3)
 
-        L = J - 1
+        for k in pending:
+            store(k[0], k[1], nc.sync)
         scale_on_scalar(L - 1, 1, 1)
-        store(L - 1, 1)
+        store(L - 1, 1, nc.sync)
         head_sums(L, 0, 0)
         head_sums(L, 0, 1)
         head_sums(L, 1, 0)
-        add_eps(L, 0)
+        add_eps(L, 0, nc.vector)
         head_sums(L, 1, 1)
         invert(L, 0)
-        add_eps(L, 1)
+        add_eps(L, 1, nc.vector)
         scale_on_scalar(L, 0, 0)
         scale_on_vector(L, 0, 1)
-        store(L, 0)
+        store(L, 0, nc.sync)
         invert(L, 1)
         scale_on_scalar(L, 1, 0)
         scale_on_vector(L, 1, 1)
-        store(L, 1)
+        store(L, 1, nc.sync)

@@ -28,9 +28,9 @@ HT = NT // DH
 E2 = S // P
 M = B * E2
 U = J * G
-CV = 208
-CS = 112
-CP = NT - CV - CS
+CV = 448
+AHEAD = 2
+RUN = 4
 
 
 def tile_multiheadattention_pa_kernel(tc, x, w, out):
@@ -44,13 +44,10 @@ def tile_multiheadattention_pa_kernel(tc, x, w, out):
         keep = ctx.enter_context(tc.tile_pool(name="keep", bufs=1))
         stat_pool = ctx.enter_context(tc.tile_pool(name="stat", bufs=3))
         res_pool = ctx.enter_context(tc.tile_pool(name="res", bufs=J * B))
-        psum = ctx.enter_context(tc.psum_pool(name="psum", bufs=7))
-        stage_pool = ctx.enter_context(tc.psum_pool(name="stagep", bufs=1))
+        psum = ctx.enter_context(tc.psum_pool(name="psum", bufs=8))
 
         ident = const.tile([P, P], F32, name="ident")
         make_identity(nc, ident[:])
-        ident_bf = const.tile([P, P], BF16, name="ident_bf")
-        make_identity(nc, ident_bf[:])
         warm_in = const.tile([P, 1], F32, name="warm_in")
         warm_out = const.tile([P, 1], F32, name="warm_out")
         nc.gpsimd.memset(warm_in[:], 0.0)
@@ -64,13 +61,15 @@ def tile_multiheadattention_pa_kernel(tc, x, w, out):
         ctx.enter_context(tc.manual_schedule())
 
         xraw = []
-        for m in range(M):
+        wraw = []
+
+        def load_x(m):
             b, e = divmod(m, E2)
             t = xraw_pool.tile([P, D], BF16, name="xraw")
             nc.sync.dma_start(out=t[:], in_=x[b].rearrange("(p e) k -> p e k", e=E2)[:, e, :])
             xraw.append(t)
-        wraw = []
-        for u in range(U):
+
+        def load_w(u):
             j, g = divmod(u, G)
             t = wraw_pool.tile([P, PACK, NT], BF16, name="wraw")
             nc.sync.dma_start(
@@ -79,7 +78,14 @@ def tile_multiheadattention_pa_kernel(tc, x, w, out):
             )
             wraw.append(t)
 
+        for u in range(AHEAD):
+            load_w(u)
         for m in range(M):
+            load_x(m)
+        for u in range(AHEAD, U):
+            load_w(u)
+
+        def prepare_x(m):
             words = xraw[m][:].bitcast(F32)
             xg = xg_pool.tile([P, G, P, PACK], BF16, name="xg", align_bytes=64)
             xg_flat = xg[:].rearrange("p g r t -> p (g r t)")
@@ -106,35 +112,17 @@ def tile_multiheadattention_pa_kernel(tc, x, w, out):
         recs = {}
         res = {}
 
-        stage = {}
-
-        def stage_on_tensor(u):
-            t = stage_pool.tile([P, 2 * NT], BF16, name="stage")
-            stage[u] = t
-            src = wraw[u][:].rearrange("p t c -> p c t")
-            for c0 in range(0, CP, P):
-                n = min(P, CP - c0)
-                nc.tensor.matmul(
-                    out=t[:, c0 * PACK : (c0 + n) * PACK].rearrange("p (c t) -> p c t", t=PACK),
-                    lhsT=ident_bf[:],
-                    rhs=src[:, CV + CS + c0 : CV + CS + c0 + n, :],
-                    start=True,
-                    stop=True,
-                )
-
         def interleave(u):
             t = wg_pool.tile([P, NT, PACK], BF16, name="wg", align_bytes=64)
             wg[u] = t
-            src = wraw[u][:].rearrange("p t c -> p c t")
-            nc.scalar.copy(
-                out=t[:, CV + CS : NT, :],
-                in_=stage[u][:, 0 : CP * PACK].rearrange("p (c t) -> p c t", t=PACK),
+            nc.vector.tensor_copy(
+                out=t[:, 0:CV, :].rearrange("p (c i) t -> p c t i", i=RUN),
+                in_=wraw[u][:, :, 0:CV].rearrange("p t (c i) -> p c t i", i=RUN),
             )
-            nc.vector.tensor_copy(out=t[:, 0:CV, :], in_=src[:, 0:CV, :])
-            for k in pending:
-                store(k[0], k[1], nc.scalar)
-            pending.clear()
-            nc.scalar.copy(out=t[:, CV : CV + CS, :], in_=src[:, CV : CV + CS, :])
+            nc.scalar.copy(
+                out=t[:, CV:NT, :].rearrange("p (c i) t -> p c t i", i=RUN),
+                in_=wraw[u][:, :, CV:NT].rearrange("p t (c i) -> p c t i", i=RUN),
+            )
 
         def quantise(u):
             j, g = divmod(u, G)
@@ -144,9 +132,9 @@ def tile_multiheadattention_pa_kernel(tc, x, w, out):
                 in_=wg[u][:].rearrange("p c t -> p (c t)"),
             )
 
-        def multiply(j, b, g):
-            for e in range(E2):
-                m = b * E2 + e
+        def multiply(u):
+            j, g = divmod(u, G)
+            for m in range(M):
                 if g == 0:
                     acc[(j, m)] = psum.tile([P, NT], F32, name="bank")
                 cols = slice(g * P, (g + 1) * P)
@@ -161,7 +149,7 @@ def tile_multiheadattention_pa_kernel(tc, x, w, out):
                 )
 
         def head_sums(j, b, e):
-            if e == 0:
+            if (j, b) not in sums:
                 sums[(j, b)] = stat_pool.tile([P, E2 * HT], F32, name="sums")
             nc.vector.tensor_reduce(
                 out=sums[(j, b)][:, e * HT : (e + 1) * HT],
@@ -170,12 +158,37 @@ def tile_multiheadattention_pa_kernel(tc, x, w, out):
                 op=ADD,
             )
 
-        def add_eps(j, b, eng):
-            eng.tensor_scalar(out=sums[(j, b)][:], in0=sums[(j, b)][:], scalar1=EPS, scalar2=None, op0=ADD)
+        def add_eps(j, b):
+            nc.vector.tensor_scalar_add(out=sums[(j, b)][:], in0=sums[(j, b)][:], scalar1=EPS)
+
+        def add_eps_on_scalar(j, b):
+            nc.scalar.activation(out=sums[(j, b)][:], in_=sums[(j, b)][:], func=COPY, bias=EPS)
 
         def invert(j, b):
             recs[(j, b)] = stat_pool.tile([P, E2 * HT], F32, name="recs")
             nc.vector.reciprocal(out=recs[(j, b)][:], in_=sums[(j, b)][:])
+
+        def sums_on_scalar(j, b, e):
+            if (j, b) not in sums:
+                sums[(j, b)] = stat_pool.tile([P, E2 * HT], F32, name="sums")
+            if (j, b) not in res:
+                res[(j, b)] = res_pool.tile([P, HT, E2, DH], F32, name="res")
+            for h in range(HT):
+                nc.scalar.activation(
+                    out=res[(j, b)][:, h, e, :],
+                    in_=acc[(j, b * E2 + e)][:, h * DH : (h + 1) * DH],
+                    func=COPY,
+                    accum_out=sums[(j, b)][:, e * HT + h : e * HT + h + 1],
+                )
+
+        def rescale_on_scalar(j, b, e, heads):
+            for h in heads:
+                nc.scalar.activation(
+                    out=res[(j, b)][:, h, e, :],
+                    in_=res[(j, b)][:, h, e, :],
+                    func=COPY,
+                    scale=recs[(j, b)][:, e * HT + h : e * HT + h + 1],
+                )
 
         def scale_on_scalar(j, b, e):
             if (j, b) not in res:
@@ -188,20 +201,20 @@ def tile_multiheadattention_pa_kernel(tc, x, w, out):
                     scale=recs[(j, b)][:, e * HT + h : e * HT + h + 1],
                 )
 
-        def scale_on_vector(j, b, e):
+        def scale_on_vector(j, b, e, h0=0, h1=HT):
             if (j, b) not in res:
                 res[(j, b)] = res_pool.tile([P, HT, E2, DH], F32, name="res")
             nc.vector.tensor_tensor(
-                out=res[(j, b)][:, :, e, :],
-                in0=acc[(j, b * E2 + e)][:].rearrange("p (h d) -> p h d", h=HT),
-                in1=recs[(j, b)][:, e * HT : (e + 1) * HT].unsqueeze(2).to_broadcast([P, HT, DH]),
+                out=res[(j, b)][:, h0:h1, e, :],
+                in0=acc[(j, b * E2 + e)][:].rearrange("p (h d) -> p h d", h=HT)[:, h0:h1, :],
+                in1=recs[(j, b)][:, e * HT + h0 : e * HT + h1].unsqueeze(2).to_broadcast([P, h1 - h0, DH]),
                 op=MULT,
             )
 
-        def store(j, b, eng):
-            eng.dma_start(
-                out=out[b, j * HT : (j + 1) * HT].rearrange("h (p e) d -> p h (e d)", e=E2),
-                in_=res[(j, b)][:].rearrange("p h e d -> p h (e d)"),
+        def store(j, b, h0=0, h1=HT):
+            nc.sync.dma_start(
+                out=out[b, j * HT + h0 : j * HT + h1].rearrange("h (p e) d -> p h (e d)", e=E2),
+                in_=res[(j, b)][:, h0:h1].rearrange("p h e d -> p h (e d)"),
             )
 
         def pair_of(step):
@@ -210,56 +223,50 @@ def tile_multiheadattention_pa_kernel(tc, x, w, out):
             k = (step - G) // 2
             return divmod(k, B) if k < J * B else None
 
-        pending = []
-        L = J - 1
-        stage_on_tensor(0)
-        interleave(0)
-        stage_on_tensor(1)
-        for u in range(U):
-            j, g = divmod(u, G)
+        for u in range(AHEAD):
+            interleave(u)
+        quantise(0)
+        for m in range(M):
+            prepare_x(m)
+        multiply(0)
+        for u in range(1, U):
+            one, two, three = pair_of(u - 1), pair_of(u - 2), pair_of(u - 3)
+            if u >= G:
+                jm = divmod(u - G, M)
+                sums_on_scalar(jm[0], jm[1] // E2, jm[1] % E2)
+            if one:
+                add_eps_on_scalar(one[0], one[1])
+            if two:
+                rescale_on_scalar(two[0], two[1], 0, range(HT))
+            if three:
+                rescale_on_scalar(three[0], three[1], 1, range(HT))
+                store(three[0], three[1])
             if u + 1 < U:
                 interleave(u + 1)
-            if u + 2 < U:
-                stage_on_tensor(u + 2)
-            now, one, two = pair_of(u), pair_of(u - 1), pair_of(u - 2)
-            if now:
-                head_sums(now[0], now[1], 0)
-                head_sums(now[0], now[1], 1)
+            quantise(u)
             if one:
                 invert(one[0], one[1])
-            quantise(u)
-            if now:
-                add_eps(now[0], now[1], nc.gpsimd)
-            if one:
-                scale_on_scalar(one[0], one[1], 0)
-            if two:
-                scale_on_scalar(two[0], two[1], 1)
-                pending.append(two)
-            multiply(j, 0, g)
-            if u >= 2 and u < U - 2:
-                multiply((u - 2) // G, 1, (u - 2) % G)
-            if u == U - 2:
-                multiply(L, 1, 0)
-                multiply(L, 1, 1)
-                multiply(L, 1, 2)
-            if u == U - 1:
-                multiply(L, 1, 3)
+            multiply(u)
 
-        for k in pending:
-            store(k[0], k[1], nc.sync)
-        scale_on_scalar(L - 1, 1, 1)
-        store(L - 1, 1, nc.sync)
+        L = J - 1
+        HH = HT // 2
+        rescale_on_scalar(L - 1, 1, 0, range(HT))
+        rescale_on_scalar(L - 1, 1, 1, range(HT))
+        store(L - 1, 1)
         head_sums(L, 0, 0)
         head_sums(L, 0, 1)
         head_sums(L, 1, 0)
-        add_eps(L, 0, nc.vector)
-        head_sums(L, 1, 1)
+        sums_on_scalar(L, 1, 1)
+        add_eps(L, 0)
+        add_eps(L, 1)
         invert(L, 0)
-        add_eps(L, 1, nc.vector)
-        scale_on_scalar(L, 0, 0)
-        scale_on_vector(L, 0, 1)
-        store(L, 0, nc.sync)
         invert(L, 1)
-        scale_on_scalar(L, 1, 0)
-        scale_on_vector(L, 1, 1)
-        store(L, 1, nc.sync)
+        scale_on_vector(L, 0, 0)
+        scale_on_scalar(L, 0, 1)
+        store(L, 0)
+        scale_on_vector(L, 1, 0, 0, HH)
+        rescale_on_scalar(L, 1, 1, range(0, HH))
+        store(L, 1, 0, HH)
+        scale_on_vector(L, 1, 0, HH, HT)
+        rescale_on_scalar(L, 1, 1, range(HH, HT))
+        store(L, 1, HH, HT)

@@ -28,8 +28,7 @@ HT = NT // DH
 E2 = S // P
 M = B * E2
 U = J * G
-CV = 448
-AHEAD = 2
+CV_OF = [320] * 5 + [352] * 2 + [472] * 9
 RUN = 4
 
 
@@ -78,14 +77,13 @@ def tile_multiheadattention_pa_kernel(tc, x, w, out):
             )
             wraw.append(t)
 
-        for u in range(AHEAD):
-            load_w(u)
         for m in range(M):
+            load_w(m)
             load_x(m)
-        for u in range(AHEAD, U):
+        for u in range(M, U):
             load_w(u)
 
-        def prepare_x(m):
+        def prepare_x(m, then_on_scalar):
             words = xraw[m][:].bitcast(F32)
             xg = xg_pool.tile([P, G, P, PACK], BF16, name="xg", align_bytes=64)
             xg_flat = xg[:].rearrange("p g r t -> p (g r t)")
@@ -100,10 +98,8 @@ def tile_multiheadattention_pa_kernel(tc, x, w, out):
                         )
                 dst = xg_words[:, 2 * half : 2 * half + 2, :, :]
                 src = bank[:].rearrange("p g u r -> p g r u")
-                if half == 0:
-                    nc.vector.tensor_copy(out=dst, in_=src)
-                else:
-                    nc.scalar.copy(out=dst, in_=src)
+                nc.scalar.copy(out=dst, in_=src)
+            interleave_on_scalar(then_on_scalar)
             nc.vector.quantize_mx(out=xc[:, m, :].bitcast(E5X4), scales=xs[:, m, :], in_=xg_flat)
 
         wg = {}
@@ -112,17 +108,22 @@ def tile_multiheadattention_pa_kernel(tc, x, w, out):
         recs = {}
         res = {}
 
-        def interleave(u):
-            t = wg_pool.tile([P, NT, PACK], BF16, name="wg", align_bytes=64)
-            wg[u] = t
+        def interleave_on_vector(u):
+            wg[u] = wg_pool.tile([P, NT, PACK], BF16, name="wg", align_bytes=64)
             nc.vector.tensor_copy(
-                out=t[:, 0:CV, :].rearrange("p (c i) t -> p c t i", i=RUN),
-                in_=wraw[u][:, :, 0:CV].rearrange("p t (c i) -> p c t i", i=RUN),
+                out=wg[u][:, 0 : CV_OF[u], :].rearrange("p (c i) t -> p c t i", i=RUN),
+                in_=wraw[u][:, :, 0 : CV_OF[u]].rearrange("p t (c i) -> p c t i", i=RUN),
             )
+
+        def interleave_on_scalar(u):
             nc.scalar.copy(
-                out=t[:, CV:NT, :].rearrange("p (c i) t -> p c t i", i=RUN),
-                in_=wraw[u][:, :, CV:NT].rearrange("p t (c i) -> p c t i", i=RUN),
+                out=wg[u][:, CV_OF[u] : NT, :],
+                in_=wraw[u][:, :, CV_OF[u] : NT].rearrange("p t c -> p c t"),
             )
+
+        def interleave(u):
+            interleave_on_vector(u)
+            interleave_on_scalar(u)
 
         def quantise(u):
             j, g = divmod(u, G)
@@ -132,9 +133,9 @@ def tile_multiheadattention_pa_kernel(tc, x, w, out):
                 in_=wg[u][:].rearrange("p c t -> p (c t)"),
             )
 
-        def multiply(u):
+        def multiply(u, tiles=range(M)):
             j, g = divmod(u, G)
-            for m in range(M):
+            for m in tiles:
                 if g == 0:
                     acc[(j, m)] = psum.tile([P, NT], F32, name="bank")
                 cols = slice(g * P, (g + 1) * P)
@@ -223,13 +224,15 @@ def tile_multiheadattention_pa_kernel(tc, x, w, out):
             k = (step - G) // 2
             return divmod(k, B) if k < J * B else None
 
-        for u in range(AHEAD):
-            interleave(u)
-        quantise(0)
+        interleave(0)
         for m in range(M):
-            prepare_x(m)
-        multiply(0)
-        for u in range(1, U):
+            quantise(m)
+            interleave_on_vector(m + 1)
+            prepare_x(m, m + 1)
+        for m in range(M):
+            for g in range(G):
+                multiply(g, [m])
+        for u in range(G, U):
             one, two, three = pair_of(u - 1), pair_of(u - 2), pair_of(u - 3)
             if u >= G:
                 jm = divmod(u - G, M)

@@ -191,10 +191,10 @@ def tile_multiheadattention_pa_kernel(tc, x, w, out):
                     scale=recs[(j, b)][:, e * HT + h : e * HT + h + 1],
                 )
 
-        def scale_on_scalar(j, b, e):
+        def scale_on_scalar(j, b, e, heads):
             if (j, b) not in res:
                 res[(j, b)] = res_pool.tile([P, HT, E2, DH], F32, name="res")
-            for h in range(HT):
+            for h in heads:
                 nc.scalar.activation(
                     out=res[(j, b)][:, h, e, :],
                     in_=acc[(j, b * E2 + e)][:, h * DH : (h + 1) * DH],
@@ -253,23 +253,23 @@ def tile_multiheadattention_pa_kernel(tc, x, w, out):
 
         L = J - 1
         HH = HT // 2
-        rescale_on_scalar(L - 1, 1, 0, range(HT))
-        rescale_on_scalar(L - 1, 1, 1, range(HT))
-        store(L - 1, 1)
+        for half in (range(0, HH), range(HH, HT)):
+            rescale_on_scalar(L - 1, 1, 0, half)
+            rescale_on_scalar(L - 1, 1, 1, half)
+            store(L - 1, 1, half.start, half.stop)
         head_sums(L, 0, 0)
         head_sums(L, 0, 1)
         head_sums(L, 1, 0)
         sums_on_scalar(L, 1, 1)
         add_eps(L, 0)
-        add_eps(L, 1)
         invert(L, 0)
-        invert(L, 1)
         scale_on_vector(L, 0, 0)
-        scale_on_scalar(L, 0, 1)
-        store(L, 0)
-        scale_on_vector(L, 1, 0, 0, HH)
-        rescale_on_scalar(L, 1, 1, range(0, HH))
-        store(L, 1, 0, HH)
-        scale_on_vector(L, 1, 0, HH, HT)
-        rescale_on_scalar(L, 1, 1, range(HH, HT))
-        store(L, 1, HH, HT)
+        add_eps(L, 1)
+        invert(L, 1)
+        for half in (range(0, HH), range(HH, HT)):
+            scale_on_scalar(L, 0, 1, half)
+            store(L, 0, half.start, half.stop)
+        for half in (range(0, HH), range(HH, HT)):
+            scale_on_vector(L, 1, 0, half.start, half.stop)
+            rescale_on_scalar(L, 1, 1, half)
+            store(L, 1, half.start, half.stop)

@@ -28,7 +28,7 @@ HT = NT // DH
 E2 = S // P
 M = B * E2
 U = J * G
-CV_OF = [320] * 5 + [352] * 2 + [472] * 9
+CV_OF = [320] * 5 + [352] * 2 + [496] * 9
 RUN = 4
 
 
@@ -117,8 +117,8 @@ def tile_multiheadattention_pa_kernel(tc, x, w, out):
 
         def interleave_on_scalar(u):
             nc.scalar.copy(
-                out=wg[u][:, CV_OF[u] : NT, :],
-                in_=wraw[u][:, :, CV_OF[u] : NT].rearrange("p t c -> p c t"),
+                out=wg[u][:, CV_OF[u] : NT, :].rearrange("p (c i) t -> p c t i", i=RUN),
+                in_=wraw[u][:, :, CV_OF[u] : NT].rearrange("p t (c i) -> p c t i", i=RUN),
             )
 
         def interleave(u):

@@ -239,20 +239,22 @@ def tile_multiheadattention_pa_kernel(tc, x, w, out):
                 sums_on_scalar(jm[0], jm[1] // E2, jm[1] % E2)
             if one:
                 add_eps_on_scalar(one[0], one[1])
-            if two:
-                rescale_on_scalar(two[0], two[1], 0, range(HT))
             if three:
                 rescale_on_scalar(three[0], three[1], 1, range(HT))
                 store(three[0], three[1])
             if u + 1 < U:
-                interleave(u + 1)
+                interleave_on_vector(u + 1)
+            if two:
+                invert(two[0], two[1])
+                rescale_on_scalar(two[0], two[1], 0, range(HT))
+            if u + 1 < U:
+                interleave_on_scalar(u + 1)
             quantise(u)
-            if one:
-                invert(one[0], one[1])
             multiply(u)
 
         L = J - 1
         HH = HT // 2
+        invert(L - 1, 1)
         for half in (range(0, HH), range(HH, HT)):
             rescale_on_scalar(L - 1, 1, 0, half)
             rescale_on_scalar(L - 1, 1, 1, half)

@@ -234,6 +234,8 @@ def tile_multiheadattention_pa_kernel(tc, x, w, out):
                 multiply(g, [m])
         for u in range(G, U):
             one, two, three = pair_of(u - 1), pair_of(u - 2), pair_of(u - 3)
+            if u + 1 < U:
+                interleave(u + 1)
             if u >= G:
                 jm = divmod(u - G, M)
                 sums_on_scalar(jm[0], jm[1] // E2, jm[1] % E2)
@@ -242,13 +244,9 @@ def tile_multiheadattention_pa_kernel(tc, x, w, out):
             if three:
                 rescale_on_scalar(three[0], three[1], 1, range(HT))
                 store(three[0], three[1])
-            if u + 1 < U:
-                interleave_on_vector(u + 1)
             if two:
                 invert(two[0], two[1])
                 rescale_on_scalar(two[0], two[1], 0, range(HT))
-            if u + 1 < U:
-                interleave_on_scalar(u + 1)
             quantise(u)
             multiply(u)
 

@@ -111,8 +111,8 @@ def tile_multiheadattention_pa_kernel(tc, x, w, out):
         def interleave_on_vector(u):
             wg[u] = wg_pool.tile([P, NT, PACK], BF16, name="wg", align_bytes=64)
             nc.vector.tensor_copy(
-                out=wg[u][:, 0 : CV_OF[u], :].rearrange("p (c i) t -> p c t i", i=RUN),
-                in_=wraw[u][:, :, 0 : CV_OF[u]].rearrange("p t (c i) -> p c t i", i=RUN),
+                out=wg[u][:, 0 : CV_OF[u], :].rearrange("p (c i) t -> p c t i", i=2),
+                in_=wraw[u][:, :, 0 : CV_OF[u]].rearrange("p t (c i) -> p c t i", i=2),
             )
 
         def interleave_on_scalar(u):

@@ -28,7 +28,7 @@ HT = NT // DH
 E2 = S // P
 M = B * E2
 U = J * G
-CV_OF = [320] * 5 + [352] * 2 + [496] * 9
+CV_OF = [320] * 5 + [352] * 2 + [480] * 9
 RUN = 4
 
 
@@ -234,13 +234,18 @@ def tile_multiheadattention_pa_kernel(tc, x, w, out):
                 multiply(g, [m])
         for u in range(G, U):
             one, two, three = pair_of(u - 1), pair_of(u - 2), pair_of(u - 3)
+            early = u < G + 2
             if u + 1 < U:
-                interleave(u + 1)
+                interleave_on_vector(u + 1)
+                if not early:
+                    interleave_on_scalar(u + 1)
             if u >= G:
                 jm = divmod(u - G, M)
                 sums_on_scalar(jm[0], jm[1] // E2, jm[1] % E2)
             if one:
                 add_eps_on_scalar(one[0], one[1])
+            if early:
+                interleave_on_scalar(u + 1)
             if three:
                 rescale_on_scalar(three[0], three[1], 1, range(HT))
                 store(three[0], three[1])

from contextlib import ExitStack

import concourse.mybir as mybir
from concourse.masks import make_identity

B, S, D, H, DH = 2, 256, 2048, 16, 128
EPS = 1e-6
FLOPS = 2 * B * S * D * H * DH

F32 = mybir.dt.float32
BF16 = mybir.dt.bfloat16
U32 = mybir.dt.uint32
U8 = mybir.dt.uint8
E4X4 = mybir.dt.float8_e4m3fn_x4
E5X4 = mybir.dt.float8_e5m2_x4
ADD = mybir.AluOpType.add
MULT = mybir.AluOpType.mult
COPY = mybir.ActivationFunctionType.Copy
AX = mybir.AxisListType.X

P = 128
PACK = 4
KP = P * PACK
G = D // KP
NT = 512
J = H * DH // NT
HT = NT // DH
E2 = S // P
M = B * E2
U = J * G
CV_OF = [320] * 5 + [352] * 2 + [480] * 9
RUN = 4


def tile_multiheadattention_pa_kernel(tc, x, w, out):
    nc = tc.nc
    with ExitStack() as ctx:
        const = ctx.enter_context(tc.tile_pool(name="const", bufs=1))
        xraw_pool = ctx.enter_context(tc.tile_pool(name="xraw", bufs=M))
        wraw_pool = ctx.enter_context(tc.tile_pool(name="wraw", bufs=U))
        xg_pool = ctx.enter_context(tc.tile_pool(name="xg", bufs=2))
        wg_pool = ctx.enter_context(tc.tile_pool(name="wg", bufs=3))
        keep = ctx.enter_context(tc.tile_pool(name="keep", bufs=1))
        stat_pool = ctx.enter_context(tc.tile_pool(name="stat", bufs=3))
        res_pool = ctx.enter_context(tc.tile_pool(name="res", bufs=J * B))
        psum = ctx.enter_context(tc.psum_pool(name="psum", bufs=8))

        ident = const.tile([P, P], F32, name="ident")
        make_identity(nc, ident[:])
        warm_in = const.tile([P, 1], F32, name="warm_in")
        warm_out = const.tile([P, 1], F32, name="warm_out")
        nc.gpsimd.memset(warm_in[:], 0.0)
        nc.scalar.activation(out=warm_out[:], in_=warm_in[:], func=COPY)

        xc = keep.tile([P, M, G * P], U32, name="xc", align_bytes=64)
        xs = keep.tile([P, M, G * P], U8, name="xs", align_bytes=64)
        wc = [keep.tile([P, G, NT], U32, name="wc%d" % j, align_bytes=64) for j in range(J)]
        ws = [keep.tile([P, G, NT], U8, name="ws%d" % j, align_bytes=64) for j in range(J)]

        ctx.enter_context(tc.manual_schedule())

        xraw = []
        wraw = []

        def load_x(m):
            b, e = divmod(m, E2)
            t = xraw_pool.tile([P, D], BF16, name="xraw")
            nc.sync.dma_start(out=t[:], in_=x[b].rearrange("(p e) k -> p e k", e=E2)[:, e, :])
            xraw.append(t)

        def load_w(u):
            j, g = divmod(u, G)
            t = wraw_pool.tile([P, PACK, NT], BF16, name="wraw")
            nc.sync.dma_start(
                out=t[:],
                in_=w[g * KP : (g + 1) * KP, j * NT : (j + 1) * NT].rearrange("(p t) c -> p t c", t=PACK),
            )
            wraw.append(t)

        for m in range(M):
            load_w(m)
            load_x(m)
        for u in range(M, U):
            load_w(u)

        def prepare_x(m, then_on_scalar):
            words = xraw[m][:].bitcast(F32)
            xg = xg_pool.tile([P, G, P, PACK], BF16, name="xg", align_bytes=64)
            xg_flat = xg[:].rearrange("p g r t -> p (g r t)")
            xg_words = xg_flat.bitcast(F32).rearrange("p (g r u) -> p g r u", g=G, u=2)
            for half in range(2):
                bank = psum.tile([P, 2, 2, P], F32, name="bank")
                for gg in range(2):
                    base = (KP // 2) * (2 * half + gg)
                    for u2 in range(2):
                        nc.tensor.transpose(
                            bank[:, gg, u2, :], words[:, base + u2 : base + KP // 2 : 2], ident[:]
                        )
                dst = xg_words[:, 2 * half : 2 * half + 2, :, :]
                src = bank[:].rearrange("p g u r -> p g r u")
                nc.scalar.copy(out=dst, in_=src)
            interleave_on_scalar(then_on_scalar)
            nc.vector.quantize_mx(out=xc[:, m, :].bitcast(E5X4), scales=xs[:, m, :], in_=xg_flat)

        wg = {}
        acc = {}
        sums = {}
        recs = {}
        res = {}

        def interleave_on_vector(u):
            wg[u] = wg_pool.tile([P, NT, PACK], BF16, name="wg", align_bytes=64)
            nc.vector.tensor_copy(
                out=wg[u][:, 0 : CV_OF[u], :].rearrange("p (c i) t -> p c t i", i=2),
                in_=wraw[u][:, :, 0 : CV_OF[u]].rearrange("p t (c i) -> p c t i", i=2),
            )

        def interleave_on_scalar(u):
            nc.scalar.copy(
                out=wg[u][:, CV_OF[u] : NT, :].rearrange("p (c i) t -> p c t i", i=RUN),
                in_=wraw[u][:, :, CV_OF[u] : NT].rearrange("p t (c i) -> p c t i", i=RUN),
            )

        def interleave(u):
            interleave_on_vector(u)
            interleave_on_scalar(u)

        def quantise(u):
            j, g = divmod(u, G)
            nc.vector.quantize_mx(
                out=wc[j][:, g, :].bitcast(E4X4),
                scales=ws[j][:, g, :],
                in_=wg[u][:].rearrange("p c t -> p (c t)"),
            )

        def multiply(u, tiles=range(M)):
            j, g = divmod(u, G)
            for m in tiles:
                if g == 0:
                    acc[(j, m)] = psum.tile([P, NT], F32, name="bank")
                cols = slice(g * P, (g + 1) * P)
                nc.tensor.matmul_mx(
                    out=acc[(j, m)][:],
                    lhsT=xc[:, m, cols].bitcast(E5X4),
                    lhsT_scale=xs[:, m, cols],
                    rhs=wc[j][:, g, :].bitcast(E4X4),
                    rhs_scale=ws[j][:, g, :],
                    start=(g == 0),
                    stop=(g == G - 1),
                )

        def head_sums(j, b, e):
            if (j, b) not in sums:
                sums[(j, b)] = stat_pool.tile([P, E2 * HT], F32, name="sums")
            nc.vector.tensor_reduce(
                out=sums[(j, b)][:, e * HT : (e + 1) * HT],
                in_=acc[(j, b * E2 + e)][:].rearrange("p (h d) -> p h d", h=HT),
                axis=AX,
                op=ADD,
            )

        def add_eps(j, b):
            nc.vector.tensor_scalar_add(out=sums[(j, b)][:], in0=sums[(j, b)][:], scalar1=EPS)

        def add_eps_on_scalar(j, b):
            nc.scalar.activation(out=sums[(j, b)][:], in_=sums[(j, b)][:], func=COPY, bias=EPS)

        def invert(j, b):
            recs[(j, b)] = stat_pool.tile([P, E2 * HT], F32, name="recs")
            nc.vector.reciprocal(out=recs[(j, b)][:], in_=sums[(j, b)][:])

        def sums_on_scalar(j, b, e):
            if (j, b) not in sums:
                sums[(j, b)] = stat_pool.tile([P, E2 * HT], F32, name="sums")
            if (j, b) not in res:
                res[(j, b)] = res_pool.tile([P, HT, E2, DH], F32, name="res")
            for h in range(HT):
                nc.scalar.activation(
                    out=res[(j, b)][:, h, e, :],
                    in_=acc[(j, b * E2 + e)][:, h * DH : (h + 1) * DH],
                    func=COPY,
                    accum_out=sums[(j, b)][:, e * HT + h : e * HT + h + 1],
                )

        def rescale_on_scalar(j, b, e, heads):
            for h in heads:
                nc.scalar.activation(
                    out=res[(j, b)][:, h, e, :],
                    in_=res[(j, b)][:, h, e, :],
                    func=COPY,
                    scale=recs[(j, b)][:, e * HT + h : e * HT + h + 1],
                )

        def scale_on_scalar(j, b, e, heads):
            if (j, b) not in res:
                res[(j, b)] = res_pool.tile([P, HT, E2, DH], F32, name="res")
            for h in heads:
                nc.scalar.activation(
                    out=res[(j, b)][:, h, e, :],
                    in_=acc[(j, b * E2 + e)][:, h * DH : (h + 1) * DH],
                    func=COPY,
                    scale=recs[(j, b)][:, e * HT + h : e * HT + h + 1],
                )

        def scale_on_vector(j, b, e, h0=0, h1=HT):
            if (j, b) not in res:
                res[(j, b)] = res_pool.tile([P, HT, E2, DH], F32, name="res")
            nc.vector.tensor_tensor(
                out=res[(j, b)][:, h0:h1, e, :],
                in0=acc[(j, b * E2 + e)][:].rearrange("p (h d) -> p h d", h=HT)[:, h0:h1, :],
                in1=recs[(j, b)][:, e * HT + h0 : e * HT + h1].unsqueeze(2).to_broadcast([P, h1 - h0, DH]),
                op=MULT,
            )

        def store(j, b, h0=0, h1=HT):
            nc.sync.dma_start(
                out=out[b, j * HT + h0 : j * HT + h1].rearrange("h (p e) d -> p h (e d)", e=E2),
                in_=res[(j, b)][:, h0:h1].rearrange("p h e d -> p h (e d)"),
            )

        def pair_of(step):
            if step < G or step % 2 == 1:
                return None
            k = (step - G) // 2
            return divmod(k, B) if k < J * B else None

        interleave(0)
        for m in range(M):
            quantise(m)
            interleave_on_vector(m + 1)
            prepare_x(m, m + 1)
        for m in range(M):
            for g in range(G):
                multiply(g, [m])
        for u in range(G, U):
            one, two, three = pair_of(u - 1), pair_of(u - 2), pair_of(u - 3)
            early = u < G + 2
            if u + 1 < U:
                interleave_on_vector(u + 1)
                if not early:
                    interleave_on_scalar(u + 1)
            if u >= G:
                jm = divmod(u - G, M)
                sums_on_scalar(jm[0], jm[1] // E2, jm[1] % E2)
            if one:
                add_eps_on_scalar(one[0], one[1])
            if early:
                interleave_on_scalar(u + 1)
            if three:
                rescale_on_scalar(three[0], three[1], 1, range(HT))
                store(three[0], three[1])
            if two:
                invert(two[0], two[1])
                rescale_on_scalar(two[0], two[1], 0, range(HT))
            quantise(u)
            multiply(u)

        L = J - 1
        HH = HT // 2
        invert(L - 1, 1)
        for half in (range(0, HH), range(HH, HT)):
            rescale_on_scalar(L - 1, 1, 0, half)
            rescale_on_scalar(L - 1, 1, 1, half)
            store(L - 1, 1, half.start, half.stop)
        head_sums(L, 0, 0)
        head_sums(L, 0, 1)
        head_sums(L, 1, 0)
        sums_on_scalar(L, 1, 1)
        add_eps(L, 0)
        invert(L, 0)
        scale_on_vector(L, 0, 0)
        add_eps(L, 1)
        invert(L, 1)
        for half in (range(0, HH), range(HH, HT)):
            scale_on_scalar(L, 0, 1, half)
            store(L, 0, half.start, half.stop)
        for half in (range(0, HH), range(HH, HT)):
            scale_on_vector(L, 1, 0, half.start, half.stop)
            rescale_on_scalar(L, 1, 1, half)
            store(L, 1, half.start, half.stop)
